import numpy as np
import ml_dtypes


def mxq(x, axis, fmt="e4m3"):
    dtype, down = {"e4m3": (ml_dtypes.float8_e4m3fn, 7), "e5m2": (ml_dtypes.float8_e5m2, 14)}[fmt]
    v = np.moveaxis(np.asarray(x, np.float32).astype(ml_dtypes.bfloat16).astype(np.float64), axis, -1)
    blocks = v.reshape(v.shape[:-1] + (-1, 32))
    amax = np.abs(blocks).max(-1, keepdims=True)
    byte = np.maximum(np.where(amax > 0, np.frexp(amax)[1] - 1 + 127, 0) - down, 1)
    scale = np.exp2(byte - 127.0)
    codes = (blocks / scale).astype(np.float32).astype(dtype).astype(np.float64)
    return np.moveaxis((codes * scale).reshape(v.shape), -1, axis)


WIDE = False


def mx_kscale(k):
    if not WIDE:
        return np.ones(k)
    levels = np.array([10, -10, 5, -5, 0])
    if k % 512:
        return np.exp2(np.random.permutation(np.resize(levels, k // 32))).repeat(32)
    a = np.empty((k // 512, 16))
    for p in range(k // 512):
        a[p, :8] = np.random.permutation(np.resize(levels, 8))
        for g in range(8):
            far = levels[np.abs(levels - a[p, g]) >= 10]
            a[p, g + 8] = far[np.random.randint(len(far))]
    return np.exp2(a.ravel()).repeat(32)


BF16 = ml_dtypes.bfloat16


def bf(x):
    return np.asarray(x, np.float32).astype(BF16)


def f64(x):
    return np.asarray(x).astype(np.float64)


E2M1 = np.array([0.0, 0.5, 1.0, 1.5, 2.0, 3.0, 4.0, 6.0, -0.0, -0.5, -1.0, -1.5, -2.0, -3.0, -4.0, -6.0])


def pack_weight(w, fmt):
    k, n = w.shape
    w = f64(bf(w)).reshape(k // 32, 32, n)
    amax = np.abs(w).max(1)
    if fmt == "e4m3":
        byte = np.frexp(amax)[1] - 1 + 127 - 7
    else:
        mant, ex = np.frexp(amax / 6.0)
        byte = np.where(mant > 0.5, ex, ex - 1) + 127
    byte = np.clip(np.where(amax > 0, byte, 1), 1, 254)
    scaled = (w * np.exp2(127.0 - byte)[:, None, :]).reshape(k, n).astype(np.float32)
    by_word = np.ascontiguousarray(scaled.reshape(k // 512, 128, 4, n).transpose(0, 1, 3, 2))
    if fmt == "e4m3":
        words = by_word.astype(ml_dtypes.float8_e4m3fn).view(np.uint8)
    else:
        c = by_word.astype(ml_dtypes.float4_e2m1fn).view(np.uint8) & 0xF
        words = c[..., 0::2] | (c[..., 1::2] << 4)
    return np.ascontiguousarray(words), np.ascontiguousarray(byte.astype(np.uint8).reshape(k // 512, 16, n))


def unpack_weight(words, scales, fmt):
    g, p, n, _ = words.shape
    if fmt == "e4m3":
        vals = np.ascontiguousarray(words).view(ml_dtypes.float8_e4m3fn).astype(np.float64)
    else:
        nib = np.empty((g, p, n, 4), np.uint8)
        nib[..., 0::2] = words & 0xF
        nib[..., 1::2] = words >> 4
        vals = E2M1[nib]
    vals = vals * np.repeat(np.exp2(scales.astype(np.float64) - 127.0), 8, axis=1)[..., None]
    return vals.transpose(0, 1, 3, 2).reshape(g * 512, n)
def pack4(w):
    words, scales = pack_weight(w, "e2m1")
    return words.reshape(words.shape[0], 128, -1), scales


def unpack4(words, scales):
    return unpack_weight(words.reshape(words.shape[0], 128, -1, 2), scales, "e2m1")


B, V, D, P, Q, R, O = 16, 16, 512, 512, 512, 1024, 512
NEG_SLOPE = 0.2


def lrelu(v):
    return np.where(v >= 0, v, NEG_SLOPE * v)


def draw0():
    s, u = mx_kscale(Q), mx_kscale(D + R)
    g = np.random.standard_normal((B, V, V, Q)) * 0.8
    h2 = bf(lrelu(g) * s)
    F = bf(np.random.standard_normal((B, V, D)) * u[:D])
    W3_words, W3_scales = pack4(np.random.standard_normal((Q, R)) * 1.5 / np.sqrt(Q) / s[:, None] * u[D:])
    b3 = bf(np.random.standard_normal(R) * 0.3 * u[D:])
    Wf_words, Wf_scales = pack4(np.random.standard_normal((D + R, O)) / np.sqrt(D + R) / u[:, None])
    b_f = bf(np.random.standard_normal(O) * 0.3)
    return {"h2": h2,
            "F": F,
            "W3_words": W3_words,
            "W3_scales": W3_scales,
            "b3": b3,
            "Wf_words": Wf_words,
            "Wf_scales": Wf_scales,
            "b_f": b_f}


def core(h2, F, W3_words, W3_scales, b3, Wf_words, Wf_scales, b_f):
    h3 = lrelu((mxq(f64(h2), 3, "e4m3") @ unpack4(W3_words, W3_scales)) + f64(b3))
    Msum = h3.sum(axis=-2)
    X = np.concatenate([f64(F), Msum], axis=-1).reshape(-1, D + R)
    return (mxq(X, 1, "e4m3") @ unpack4(Wf_words, Wf_scales)) + f64(b_f)


def e4m3fn_bytes(y):
    return np.clip(np.asarray(y, np.float64), -448.0, 448.0).astype(np.float32).astype(ml_dtypes.float8_e4m3fn).view(np.uint8)


def e4m3fn_values(b):
    return np.asarray(b, np.uint8).view(ml_dtypes.float8_e4m3fn).astype(np.float64)


def setup_inputs():
    d = draw0()
    x0 = np.asarray(d['h2']).astype(np.float64)
    s = (np.max(np.abs(x0), axis=(0, 1, 2), keepdims=True) / 448.0).astype(np.float32)
    out = {}
    for k, v in d.items():
        if k == 'h2':
            out['h2_bytes'] = e4m3fn_bytes(x0 / s.astype(np.float64))
            out['h2_scale'] = s
        else:
            out[k] = v
    return out


def reference(h2_bytes, h2_scale, F, W3_words, W3_scales, b3, Wf_words, Wf_scales, b_f):
    return core(e4m3fn_values(h2_bytes) * h2_scale.astype(np.float64), F, W3_words, W3_scales, b3, Wf_words, Wf_scales, b_f)

@@ -1,0 +1,288 @@
+from contextlib import ExitStack
+
+import concourse.mybir as mybir
+from concourse.masks import make_identity
+
+F32 = mybir.dt.float32
+BF16 = mybir.dt.bfloat16
+U32 = mybir.dt.uint32
+I32 = mybir.dt.int32
+U8 = mybir.dt.uint8
+FP8 = mybir.dt.float8_e4m3fn
+FP8X4 = mybir.dt.float8_e4m3fn_x4
+FP4X4 = mybir.dt.float4_e2m1fn_x4
+ADD = mybir.AluOpType.add
+MULT = mybir.AluOpType.mult
+MAX = mybir.AluOpType.max
+RELU = mybir.ActivationFunctionType.Relu
+IDENT = mybir.ActivationFunctionType.Identity
+AXX = mybir.AxisListType.X
+
+FLOPS = 2 * 4096 * 512 * 1024 + 2 * 256 * 1536 * 512
+
+
+def tile_nonlocalmp_pb_t_w4_kernel(tc, h2_bytes, h2_scale, F, W3_words, W3_scales, b3, Wf_words, Wf_scales, b_f, out):
+    nc = tc.nc
+    h2 = h2_bytes.rearrange("b i j k -> (b i) (j k)")
+    f_rows = F.rearrange("b i d -> (b i) d")
+
+    with ExitStack() as ctx:
+        keep = ctx.enter_context(tc.tile_pool(name="keep", bufs=1))
+        work = ctx.enter_context(tc.tile_pool(name="work", bufs=3))
+        ptr = ctx.enter_context(tc.psum_pool(name="ptr", bufs=2))
+        pmm = ctx.enter_context(tc.psum_pool(name="pmm", bufs=4))
+        paux = ctx.enter_context(tc.psum_pool(name="paux", bufs=2))
+        ctx.enter_context(tc.manual_schedule())
+
+        raw = [keep.tile([128, 2048], U8, name=f"raw{w}", align_bytes=64) for w in range(8)]
+        hq = [keep.tile([128, 512], U32, name=f"hq{w}", align_bytes=64) for w in range(8)]
+        hs = [keep.tile([128, 512], U8, name=f"hs{w}", align_bytes=64) for w in range(8)]
+        w3raw = keep.tile([128, 2048], U8, name="w3raw", align_bytes=64)
+        w3sraw = keep.tile([128, 1024], U8, name="w3sraw", align_bytes=64)
+        w3 = [keep.tile([128, 1024], U8, name=f"w3_{g}", align_bytes=64) for g in range(2)]
+        w3s = [keep.tile([128, 512], U8, name=f"w3s_{g}", align_bytes=64) for g in range(2)]
+        wf = keep.tile([128, 3, 1024], U8, name="wf", align_bytes=64)
+        wfs = keep.tile([128, 3, 512], U8, name="wfs", align_bytes=64)
+        sc = keep.tile([128, 4], F32, name="sc")
+        b3t = keep.tile([128, 8], BF16, name="b3t")
+        bpos = keep.tile([128, 8], F32, name="bpos")
+        bneg = keep.tile([128, 8], F32, name="bneg")
+        cb = keep.tile([128, 8], F32, name="cb")
+        bft = keep.tile([128, 512], BF16, name="bft")
+        ft = [keep.tile([128, 512], BF16, name=f"ft{h}", align_bytes=64) for h in range(2)]
+        fx = keep.tile([128, 1024], BF16, name="fx", align_bytes=64)
+        xq0 = keep.tile([128, 256], U32, name="xq0", align_bytes=64)
+        xs0 = keep.tile([128, 256], U8, name="xs0", align_bytes=64)
+        ident = keep.tile([128, 128], F32, name="ident")
+        warm = keep.tile([128, 1], F32, name="warm")
+
+        nc.vector.memset(w3sraw[:].bitcast(I32), 0)
+        nc.gpsimd.memset(warm[:], 0.0)
+        make_identity(nc, ident[:])
+        nc.gpsimd.memset(wfs[:].rearrange("p g n -> p (g n)").bitcast(I32), 0)
+        nc.scalar.dma_start(out=sc[:], in_=h2_scale.rearrange("a b c (p t) -> p (a b c t)", t=4))
+        nc.scalar.dma_start(out=b3t[:].rearrange("p (g t) -> p g t", t=4), in_=b3.rearrange("(g p t) -> p g t", g=2, t=4))
+        nc.scalar.activation(out=warm[:], in_=warm[:], func=RELU)
+
+        def load(w):
+            h, q = w // 4, w % 4
+            nc.sync.dma_start(out=raw[w][:], in_=h2[128 * h:128 * h + 128, 2048 * q:2048 * q + 2048])
+
+        load(0)
+        for qq in range(4):
+            nc.sync.dma_start(out=w3sraw[32 * qq:32 * qq + 4, :].bitcast(I32), in_=W3_scales[0, 4 * qq:4 * qq + 4, :].bitcast(I32))
+        nc.sync.dma_start(out=w3raw[:], in_=W3_words[0])
+        for w in range(1, 8):
+            load(w)
+        for h in range(2):
+            nc.sync.dma_start(out=ft[h][:], in_=f_rows[128 * h:128 * h + 128, :])
+        nc.sync.dma_start(out=wf[:], in_=Wf_words.rearrange("g p n -> p g n"))
+        for qq in range(4):
+            nc.sync.dma_start(out=wfs[32 * qq:32 * qq + 4, :, :].bitcast(I32), in_=Wf_scales[:, 4 * qq:4 * qq + 4, :].rearrange("g q n -> q g n").bitcast(I32))
+        nc.sync.dma_start(out=bft[:], in_=b_f.partition_broadcast(128))
+
+        nc.vector.tensor_copy(out=bpos[:], in_=b3t[:])
+        nc.vector.tensor_scalar(out=bneg[:], in0=b3t[:], scalar1=-1.0, scalar2=None, op0=MULT)
+        nc.vector.tensor_scalar(out=cb[:], in0=b3t[:], scalar1=9.6, scalar2=None, op0=MULT)
+
+        wide, hb, tp = {}, {}, {}
+
+        def cast(w, c, eng):
+            wide[w, c] = work.tile([128, 1024], BF16, name="wide", align_bytes=64, bufs=4)
+            src = raw[w][:, 1024 * c:1024 * c + 1024].bitcast(FP8)
+            if eng == "v":
+                nc.vector.tensor_copy(out=wide[w, c][:], in_=src)
+            else:
+                nc.scalar.copy(out=wide[w, c][:], in_=src)
+
+        def tr(w, c):
+            tp[w, c] = ptr.tile([128, 512], F32, name="tp")
+            words = wide[w, c][:].bitcast(F32)
+            for jj in range(2):
+                for u in range(2):
+                    nc.tensor.transpose(tp[w, c][:, 256 * u + 128 * jj:256 * u + 128 * jj + 128], words[:, 256 * jj + u:256 * jj + 256:2], ident[:])
+
+        def mul(w, c):
+            if c == 0:
+                hb[w] = work.tile([128, 2048], BF16, name="hb", align_bytes=64, bufs=3)
+            nc.vector.tensor_tensor(
+                out=hb[w][:, 1024 * c:1024 * c + 1024].rearrange("p (r u e) -> p r u e", u=2, e=2),
+                in0=tp[w, c][:].bitcast(BF16).rearrange("p (u r e) -> p r u e", u=2, e=2),
+                in1=sc[:].rearrange("p (u e) -> p u e", u=2).unsqueeze(1).to_broadcast([128, 256, 2, 2]),
+                op=MULT)
+
+        def qz(w):
+            nc.vector.quantize_mx(out=hq[w][:].bitcast(FP8X4), scales=hs[w][:], in_=hb[w][:])
+
+        def w3_tile(rt):
+            g, t = rt // 4, rt % 4
+            return w3[g][:, 256 * t:256 * t + 256].bitcast(FP4X4), w3s[g][:, 128 * t:128 * t + 128]
+
+        mm, wv, cv, dv, F2, Lb, Lc, Lc2 = {}, {}, {}, {}, {}, {}, {}, {}
+
+        def main(w, rt):
+            mm[w, rt] = pmm.tile([128, 512], F32, name="mm")
+            lw, ls = w3_tile(rt)
+            nc.tensor.matmul_mx(out=mm[w, rt][:], lhsT=lw, lhsT_scale=ls, rhs=hq[w][:].bitcast(FP8X4), rhs_scale=hs[w][:], start=True, stop=True)
+
+        def evac_s(w, rt):
+            wv[w, rt] = work.tile([128, 512], F32, name=f"wv{rt}", bufs=2)
+            nc.scalar.activation(out=wv[w, rt][:], in_=mm[w, rt][:], func=RELU, bias=bpos[:, rt:rt + 1])
+
+        def evac_v(w, rt):
+            h, q = w // 4, w % 4
+            if q == 1:
+                cv[h, rt] = work.tile([128, 512], F32, name=f"cv{rt}", bufs=2)
+                o, i1 = cv[h, rt], wv[w - 1, rt]
+            else:
+                dv[h, rt] = work.tile([128, 512], F32, name=f"dv{rt % 4}", bufs=2)
+                o, i1 = dv[h, rt], cv[h, rt]
+            nc.vector.scalar_tensor_tensor(out=o[:], in0=mm[w, rt][:], scalar=bneg[:, rt:rt + 1], in1=i1[:], op0=MAX, op1=ADD)
+
+        def merge_g(w, rt):
+            h = w // 4
+            nc.gpsimd.tensor_tensor(out=cv[h, rt][:], in0=cv[h, rt][:], in1=wv[w, rt][:], op=ADD)
+
+        def f2_tile(h, rt):
+            g = rt // 4
+            if (h, g) not in F2:
+                F2[h, g] = work.tile([128, 512], F32, name=f"F2{g}", bufs=2)
+            return F2[h, g][:, 128 * (rt % 4):128 * (rt % 4) + 128]
+
+        def fold_g(h, rt):
+            d = dv[h, rt]
+            nc.gpsimd.tensor_tensor(out=d[:, 0:256], in0=d[:, 0:256], in1=d[:, 256:512], op=ADD)
+            nc.gpsimd.tensor_tensor(out=f2_tile(h, rt), in0=d[:, 0:128], in1=d[:, 128:256], op=ADD)
+
+        def fold_v(h, rt):
+            nc.vector.tensor_reduce(out=f2_tile(h, rt), in_=dv[h, rt][:].rearrange("p (j b) -> p b j", j=4), axis=AXX, op=ADD)
+
+        def lin(m, rt):
+            g, t = rt // 4, rt % 4
+            if t == 0:
+                Lb[m, g] = paux.tile([128, 512], F32, name="aux")
+            lw, ls = w3_tile(rt)
+            for n in range(8):
+                w, j = 2 * m + n // 4, n % 4
+                nc.tensor.matmul_mx(out=Lb[m, g][:, 128 * t:128 * t + 128], lhsT=lw, lhsT_scale=ls,
+                                    rhs=hq[w][:, 128 * j:128 * j + 128].bitcast(FP8X4), rhs_scale=hs[w][:, 128 * j:128 * j + 128],
+                                    start=(n == 0), stop=(n == 7))
+
+        def lin_evac(m, g):
+            h = m // 2
+            if m % 2 == 0:
+                Lc[h, g] = work.tile([128, 512], F32, name=f"Lc{g}", bufs=2)
+                for t in range(4):
+                    nc.scalar.activation(out=Lc[h, g][:, 128 * t:128 * t + 128], in_=Lb[m, g][:, 128 * t:128 * t + 128], func=IDENT, bias=cb[:, 4 * g + t:4 * g + t + 1], scale=0.2)
+            else:
+                Lc2[h, g] = work.tile([128, 512], F32, name=f"Lcc{g}", bufs=2)
+                nc.vector.scalar_tensor_tensor(out=Lc2[h, g][:], in0=Lb[m, g][:], scalar=0.2, in1=Lc[h, g][:], op0=MULT, op1=ADD)
+
+        xb, xq, xs, po = {}, {}, {}, {}
+
+        def make_x(h, g):
+            xb[h, g] = work.tile([128, 512], BF16, name="xb", align_bytes=64, bufs=2)
+            nc.vector.scalar_tensor_tensor(
+                out=xb[h, g][:].rearrange("p (b t) -> p b t", t=4),
+                in0=F2[h, g][:].rearrange("p (t b) -> p b t", t=4), scalar=0.8,
+                in1=Lc2[h, g][:].rearrange("p (t b) -> p b t", t=4), op0=MULT, op1=ADD)
+
+        def quant_x(h, g):
+            xq[h, g] = work.tile([128, 128], U32, name="xq", align_bytes=64, bufs=4)
+            xs[h, g] = work.tile([128, 128], U8, name="xs", align_bytes=64, bufs=4)
+            nc.vector.quantize_mx(out=xq[h, g][:].bitcast(FP8X4), scales=xs[h, g][:], in_=xb[h, g][:])
+
+        def final_pass(h, g):
+            if g == 0:
+                po[h] = paux.tile([128, 512], F32, name="aux")
+                lw, ls = xq0[:, 128 * h:128 * h + 128], xs0[:, 128 * h:128 * h + 128]
+            else:
+                lw, ls = xq[h, g - 1][:], xs[h, g - 1][:]
+            nc.tensor.matmul_mx(out=po[h][:], lhsT=lw.bitcast(FP8X4), lhsT_scale=ls, rhs=wf[:, g, :].bitcast(FP4X4), rhs_scale=wfs[:, g, :], start=(g == 0), stop=(g == 2))
+
+        def store(h):
+            o = work.tile([128, 512], F32, name="o", bufs=2)
+            nc.vector.tensor_tensor(out=o[:], in0=po[h][:], in1=bft[:], op=ADD)
+            nc.sync.dma_start(out=out[128 * h:128 * h + 128, :], in_=o[:])
+
+        def f_part():
+            t = ptr.tile([128, 512], F32, name="tp")
+            for h in range(2):
+                words = ft[h][:].bitcast(F32)
+                for u in range(2):
+                    nc.tensor.transpose(t[:, 256 * u + 128 * h:256 * u + 128 * h + 128], words[:, u:256:2], ident[:])
+            nc.scalar.copy(out=fx[:].bitcast(F32).rearrange("p (r u) -> p r u", u=2), in_=t[:].rearrange("p (u r) -> p r u", u=2))
+
+        def permute(g, eng):
+            eng.tensor_copy(out=w3[g][:].rearrange("p (t m e) -> p t m e", t=4, e=2), in_=w3raw[:, 1024 * g:1024 * g + 1024].rearrange("p (m t e) -> p t m e", t=4, e=2))
+
+        def permute_s(g, eng):
+            eng.tensor_copy(out=w3s[g][:].rearrange("p (t m) -> p t m", t=4), in_=w3sraw[:, 512 * g:512 * g + 512].rearrange("p (m t) -> p t m", t=4))
+
+        permute_s(0, nc.gpsimd)
+        permute(1, nc.gpsimd)
+        permute_s(1, nc.gpsimd)
+        cast(0, 0, "s")
+        cast(0, 1, "v")
+        tr(0, 0)
+        tr(0, 1)
+        permute(0, nc.vector)
+
+        for s in range(10):
+            sa, ha = 2 * ((s - 1) // 2), (s - 1) % 2
+            sb, hbk = 2 * ((s - 2) // 2) + 1, s % 2
+            m = (s - 2) // 2
+            has_a = 1 <= s <= 8
+            has_b = 2 <= s <= 9
+            fe = s < 8
+            nx = s + 1 if s + 1 < 8 else None
+            for i in range(4):
+                ra, rb = 4 * ha + i, 4 * hbk + i
+                if has_a:
+                    main(sa, ra)
+                if has_b:
+                    main(sb, rb)
+                    lin(m, rb)
+                if nx is not None and i < 2:
+                    cast(nx, i, "s")
+                if nx is not None and i >= 2:
+                    tr(nx, i - 2)
+                if s == 3 and i == 3:
+                    f_part()
+                if has_a:
+                    evac_s(sa, ra)
+                    if sa % 4 == 2:
+                        merge_g(sa, ra)
+                if fe and i < 2:
+                    mul(s, i)
+                if fe and i == 3:
+                    qz(s)
+                if has_b:
+                    evac_v(sb, rb)
+                    if sb % 4 == 3:
+                        if sb < 4:
+                            fold_g(0, rb)
+                        else:
+                            fold_v(1, rb)
+            if has_b:
+                lin_evac(m, hbk)
+            if s == 4:
+                nc.vector.quantize_mx(out=xq0[:].bitcast(FP8X4), scales=xs0[:], in_=fx[:])
+            if s == 6:
+                make_x(0, 0)
+            if s == 7:
+                quant_x(0, 0)
+                make_x(0, 1)
+            if s == 8:
+                quant_x(0, 1)
+                for g in range(3):
+                    final_pass(0, g)
+                store(0)
+                make_x(1, 0)
+            if s == 9:
+                quant_x(1, 0)
+                make_x(1, 1)
+                quant_x(1, 1)
+                for g in range(3):
+                    final_pass(1, g)
+                store(1)

@@ -15,274 +15,354 @@ ADD = mybir.AluOpType.add
 MULT = mybir.AluOpType.mult
 MAX = mybir.AluOpType.max
 RELU = mybir.ActivationFunctionType.Relu
-IDENT = mybir.ActivationFunctionType.Identity
-AXX = mybir.AxisListType.X
 
 FLOPS = 2 * 4096 * 512 * 1024 + 2 * 256 * 1536 * 512
+
+P = 128
+HALVES = 2
+CHUNKS = 8
+TILES = 8
+GROUPS = 2
+BANK = 512
+BANKS = 8
+
+SLOPE = 0.2
+RELU_SHARE = 1.0 - SLOPE
+B3_SHARE = SLOPE * 16 + RELU_SHARE * 8
+
+BEHIND = 0.0
+
+
+def text_order(work):
+    when = {}
+    left = work
+    while left:
+        blocked = []
+        for piece in left:
+            if all(name in when for name in piece["needs"]):
+                when[piece["name"]] = max([piece["when"]] + [when[name] + 0.001 for name in piece["needs"]])
+            else:
+                blocked.append(piece)
+        left = blocked
+    return sorted(work, key=lambda piece: when[piece["name"]])
 
 
 def tile_nonlocalmp_pb_t_w4_kernel(tc, h2_bytes, h2_scale, F, W3_words, W3_scales, b3, Wf_words, Wf_scales, b_f, out):
     nc = tc.nc
-    h2 = h2_bytes.rearrange("b i j k -> (b i) (j k)")
+    h2_rows = h2_bytes.rearrange("b i j k -> (b i) (j k)")
     f_rows = F.rearrange("b i d -> (b i) d")
 
     with ExitStack() as ctx:
-        keep = ctx.enter_context(tc.tile_pool(name="keep", bufs=1))
-        work = ctx.enter_context(tc.tile_pool(name="work", bufs=3))
-        ptr = ctx.enter_context(tc.psum_pool(name="ptr", bufs=2))
-        pmm = ctx.enter_context(tc.psum_pool(name="pmm", bufs=4))
-        paux = ctx.enter_context(tc.psum_pool(name="paux", bufs=2))
+        sbuf = ctx.enter_context(tc.tile_pool(name="sbuf", bufs=1))
+        psum = ctx.enter_context(tc.psum_pool(name="psum", bufs=BANKS))
         ctx.enter_context(tc.manual_schedule())
 
-        raw = [keep.tile([128, 2048], U8, name=f"raw{w}", align_bytes=64) for w in range(8)]
-        hq = [keep.tile([128, 512], U32, name=f"hq{w}", align_bytes=64) for w in range(8)]
-        hs = [keep.tile([128, 512], U8, name=f"hs{w}", align_bytes=64) for w in range(8)]
-        w3raw = keep.tile([128, 2048], U8, name="w3raw", align_bytes=64)
-        w3sraw = keep.tile([128, 1024], U8, name="w3sraw", align_bytes=64)
-        w3 = [keep.tile([128, 1024], U8, name=f"w3_{g}", align_bytes=64) for g in range(2)]
-        w3s = [keep.tile([128, 512], U8, name=f"w3s_{g}", align_bytes=64) for g in range(2)]
-        wf = keep.tile([128, 3, 1024], U8, name="wf", align_bytes=64)
-        wfs = keep.tile([128, 3, 512], U8, name="wfs", align_bytes=64)
-        sc = keep.tile([128, 4], F32, name="sc")
-        b3t = keep.tile([128, 8], BF16, name="b3t")
-        bpos = keep.tile([128, 8], F32, name="bpos")
-        bneg = keep.tile([128, 8], F32, name="bneg")
-        cb = keep.tile([128, 8], F32, name="cb")
-        bft = keep.tile([128, 512], BF16, name="bft")
-        ft = [keep.tile([128, 512], BF16, name=f"ft{h}", align_bytes=64) for h in range(2)]
-        fx = keep.tile([128, 1024], BF16, name="fx", align_bytes=64)
-        xq0 = keep.tile([128, 256], U32, name="xq0", align_bytes=64)
-        xs0 = keep.tile([128, 256], U8, name="xs0", align_bytes=64)
-        ident = keep.tile([128, 128], F32, name="ident")
-        warm = keep.tile([128, 1], F32, name="warm")
+        h2_codes = [sbuf.tile([P, 2048], U8, name=f"h2_codes{w}", align_bytes=64) for w in range(CHUNKS)]
+        hq = [sbuf.tile([P, 512], U32, name=f"hq{w}", align_bytes=64) for w in range(CHUNKS)]
+        hq_scale = [sbuf.tile([P, 512], U8, name=f"hq_scale{w}", align_bytes=64) for w in range(CHUNKS)]
+        w3 = sbuf.tile([P, 2048], U8, name="w3", align_bytes=64)
+        w3_scale = sbuf.tile([P, 1024], U8, name="w3_scale", align_bytes=64)
+        wf = sbuf.tile([P, 3, 1024], U8, name="wf", align_bytes=64)
+        wf_scale = sbuf.tile([P, 3, 512], U8, name="wf_scale", align_bytes=64)
+        k_scale = sbuf.tile([P, 4], F32, name="k_scale")
+        b3_rows = sbuf.tile([P, P], BF16, name="b3_rows")
+        b3_rows_f32 = sbuf.tile([P, P], F32, name="b3_rows_f32")
+        b3_column = sbuf.tile([P, TILES], F32, name="b3_column")
+        b3_minus = sbuf.tile([P, TILES], F32, name="b3_minus")
+        b3_spread = sbuf.tile([P, 1024], BF16, name="b3_spread")
+        b3_share = sbuf.tile([P, 1024], F32, name="b3_share")
+        b_f_spread = sbuf.tile([P, 512], BF16, name="b_f_spread")
+        f_half = [sbuf.tile([P, 512], BF16, name=f"f_half{h}", align_bytes=64) for h in range(HALVES)]
+        f_turned = sbuf.tile([P, 1024], BF16, name="f_turned", align_bytes=64)
+        fq = sbuf.tile([P, 256], U32, name="fq", align_bytes=64)
+        fq_scale = sbuf.tile([P, 256], U8, name="fq_scale", align_bytes=64)
+        identity = sbuf.tile([P, P], F32, name="identity")
+        dummy = sbuf.tile([P, 1], F32, name="dummy")
 
-        nc.vector.memset(w3sraw[:].bitcast(I32), 0)
-        nc.gpsimd.memset(warm[:], 0.0)
-        make_identity(nc, ident[:])
-        nc.gpsimd.memset(wfs[:].rearrange("p g n -> p (g n)").bitcast(I32), 0)
-        nc.scalar.dma_start(out=sc[:], in_=h2_scale.rearrange("a b c (p t) -> p (a b c t)", t=4))
-        nc.scalar.dma_start(out=b3t[:].rearrange("p (g t) -> p g t", t=4), in_=b3.rearrange("(g p t) -> p g t", g=2, t=4))
-        nc.scalar.activation(out=warm[:], in_=warm[:], func=RELU)
+        nc.vector.memset(w3_scale[:].bitcast(I32), 0)
+        make_identity(nc, identity[:])
+        nc.vector.memset(dummy[:], 0.0)
+        nc.gpsimd.memset(wf_scale[:].rearrange("p g n -> p (g n)").bitcast(I32), 0)
+        nc.scalar.dma_start(out=k_scale[:], in_=h2_scale.rearrange("a b c (p t) -> p (a b c t)", t=4))
+        nc.vector.memset(b3_rows[:], 0.0)
+        nc.scalar.dma_start(out=b3_rows[0:TILES, :], in_=b3.rearrange("(r p) -> r p", p=P))
+        nc.scalar.activation(out=dummy[:], in_=dummy[:], func=RELU)
 
-        def load(w):
+        def load_h2(w, lo, hi):
             h, q = w // 4, w % 4
-            nc.sync.dma_start(out=raw[w][:], in_=h2[128 * h:128 * h + 128, 2048 * q:2048 * q + 2048])
+            nc.sync.dma_start(out=h2_codes[w][:, lo:hi], in_=h2_rows[P * h : P * h + P, 2048 * q + lo : 2048 * q + hi])
 
-        load(0)
-        for qq in range(4):
-            nc.sync.dma_start(out=w3sraw[32 * qq:32 * qq + 4, :].bitcast(I32), in_=W3_scales[0, 4 * qq:4 * qq + 4, :].bitcast(I32))
-        nc.sync.dma_start(out=w3raw[:], in_=W3_words[0])
-        for w in range(1, 8):
-            load(w)
-        for h in range(2):
-            nc.sync.dma_start(out=ft[h][:], in_=f_rows[128 * h:128 * h + 128, :])
+        load_h2(0, 0, 1024)
+        load_h2(0, 1024, 2048)
+        for Q in range(4):
+            nc.sync.dma_start(out=w3_scale[32 * Q : 32 * Q + 4, :].bitcast(I32), in_=W3_scales[0, 4 * Q : 4 * Q + 4, :].bitcast(I32))
+        nc.sync.dma_start(out=w3[:], in_=W3_words[0])
+        for h in range(HALVES):
+            nc.sync.dma_start(out=f_half[h][:], in_=f_rows[P * h : P * h + P, :])
+        for w in range(1, CHUNKS):
+            load_h2(w, 0, 2048)
         nc.sync.dma_start(out=wf[:], in_=Wf_words.rearrange("g p n -> p g n"))
-        for qq in range(4):
-            nc.sync.dma_start(out=wfs[32 * qq:32 * qq + 4, :, :].bitcast(I32), in_=Wf_scales[:, 4 * qq:4 * qq + 4, :].rearrange("g q n -> q g n").bitcast(I32))
-        nc.sync.dma_start(out=bft[:], in_=b_f.partition_broadcast(128))
+        for Q in range(4):
+            nc.sync.dma_start(
+                out=wf_scale[32 * Q : 32 * Q + 4, :, :].bitcast(I32),
+                in_=Wf_scales[:, 4 * Q : 4 * Q + 4, :].rearrange("g q n -> q g n").bitcast(I32),
+            )
+        nc.sync.dma_start(out=b3_spread[:], in_=b3.partition_broadcast(P))
+        nc.sync.dma_start(out=b_f_spread[:], in_=b_f.partition_broadcast(P))
 
-        nc.vector.tensor_copy(out=bpos[:], in_=b3t[:])
-        nc.vector.tensor_scalar(out=bneg[:], in0=b3t[:], scalar1=-1.0, scalar2=None, op0=MULT)
-        nc.vector.tensor_scalar(out=cb[:], in0=b3t[:], scalar1=9.6, scalar2=None, op0=MULT)
+        work = []
 
-        wide, hb, tp = {}, {}, {}
+        def add(name, needs, run, when=BEHIND):
+            work.append({"name": name, "needs": needs, "when": when, "run": run})
 
-        def cast(w, c, eng):
-            wide[w, c] = work.tile([128, 1024], BF16, name="wide", align_bytes=64, bufs=4)
-            src = raw[w][:, 1024 * c:1024 * c + 1024].bitcast(FP8)
-            if eng == "v":
-                nc.vector.tensor_copy(out=wide[w, c][:], in_=src)
-            else:
-                nc.scalar.copy(out=wide[w, c][:], in_=src)
+        banks = {}
 
-        def tr(w, c):
-            tp[w, c] = ptr.tile([128, 512], F32, name="tp")
-            words = wide[w, c][:].bitcast(F32)
-            for jj in range(2):
-                for u in range(2):
-                    nc.tensor.transpose(tp[w, c][:, 256 * u + 128 * jj:256 * u + 128 * jj + 128], words[:, 256 * jj + u:256 * jj + 256:2], ident[:])
+        def bank(name):
+            if name not in banks:
+                banks[name] = psum.tile([P, BANK], F32, name="bank")
+            return banks[name]
 
-        def mul(w, c):
-            if c == 0:
-                hb[w] = work.tile([128, 2048], BF16, name="hb", align_bytes=64, bufs=3)
-            nc.vector.tensor_tensor(
-                out=hb[w][:, 1024 * c:1024 * c + 1024].rearrange("p (r u e) -> p r u e", u=2, e=2),
-                in0=tp[w, c][:].bitcast(BF16).rearrange("p (u r e) -> p r u e", u=2, e=2),
-                in1=sc[:].rearrange("p (u e) -> p u e", u=2).unsqueeze(1).to_broadcast([128, 256, 2, 2]),
-                op=MULT)
+        def spread_b3_share():
+            nc.gpsimd.tensor_scalar(out=b3_share[:], in0=b3_spread[:], scalar1=B3_SHARE, scalar2=0.0, op0=MULT, op1=ADD)
 
-        def qz(w):
-            nc.vector.quantize_mx(out=hq[w][:].bitcast(FP8X4), scales=hs[w][:], in_=hb[w][:])
+        def widen_b3_rows():
+            nc.vector.tensor_copy(out=b3_rows_f32[:], in_=b3_rows[:])
 
-        def w3_tile(rt):
-            g, t = rt // 4, rt % 4
-            return w3[g][:, 256 * t:256 * t + 256].bitcast(FP4X4), w3s[g][:, 128 * t:128 * t + 128]
+        def turn_b3_rows():
+            nc.tensor.transpose(bank("b3")[:, 0:P], b3_rows_f32[:], identity[:])
 
-        mm, wv, cv, dv, F2, Lb, Lc, Lc2 = {}, {}, {}, {}, {}, {}, {}, {}
+        def empty_b3_bank():
+            nc.vector.tensor_copy(out=b3_column[:], in_=banks["b3"][:, 0:TILES])
+            nc.vector.tensor_scalar(out=b3_minus[:], in0=banks["b3"][:, 0:TILES], scalar1=-1.0, scalar2=None, op0=MULT)
 
-        def main(w, rt):
-            mm[w, rt] = pmm.tile([128, 512], F32, name="mm")
-            lw, ls = w3_tile(rt)
-            nc.tensor.matmul_mx(out=mm[w, rt][:], lhsT=lw, lhsT_scale=ls, rhs=hq[w][:].bitcast(FP8X4), rhs_scale=hs[w][:], start=True, stop=True)
+        add("b3_share", [], spread_b3_share)
+        add("b3_widened", [("quantised", 0, 0)], widen_b3_rows)
+        add("b3_turned", ["b3_widened"], turn_b3_rows)
+        add("b3", ["b3_turned"], empty_b3_bank)
 
-        def evac_s(w, rt):
-            wv[w, rt] = work.tile([128, 512], F32, name=f"wv{rt}", bufs=2)
-            nc.scalar.activation(out=wv[w, rt][:], in_=mm[w, rt][:], func=RELU, bias=bpos[:, rt:rt + 1])
+        wide, scaled = {}, {}
+        for w in range(CHUNKS):
+            n_pieces = 4 if w == 0 else 2
+            n_j = 4 // n_pieces
+            for c in range(n_pieces):
+                lo, hi = 512 * n_j * c, 512 * n_j * (c + 1)
 
-        def evac_v(w, rt):
+                def widen(w=w, c=c, lo=lo, hi=hi):
+                    wide[w, c] = sbuf.tile([P, hi - lo], BF16, name=f"wide{w}_{c}", align_bytes=64)
+                    codes = h2_codes[w][:, lo:hi].bitcast(FP8)
+                    if w == 0 and c % 2 == 0:
+                        nc.vector.tensor_copy(out=wide[w, c][:], in_=codes)
+                    else:
+                        nc.scalar.copy(out=wide[w, c][:], in_=codes)
+
+                def turn(w=w, c=c, n_j=n_j):
+                    words = wide[w, c][:].bitcast(F32)
+                    for j in range(n_j):
+                        for u in range(2):
+                            at = P * (n_j * u + j)
+                            nc.tensor.transpose(bank(("turned", w, c))[:, at : at + P], words[:, 256 * j + u : 256 * j + 256 : 2], identity[:])
+
+                def scale(w=w, c=c, lo=lo, hi=hi, n_j=n_j):
+                    if c == 0:
+                        scaled[w] = sbuf.tile([P, 2048], BF16, name=f"scaled{w}", align_bytes=64)
+                    nc.vector.tensor_tensor(
+                        out=scaled[w][:, lo:hi].rearrange("p (n u e) -> p n u e", u=2, e=2),
+                        in0=banks["turned", w, c][:, 0 : 256 * n_j].bitcast(BF16).rearrange("p (u n e) -> p n u e", u=2, e=2),
+                        in1=k_scale[:].rearrange("p (u e) -> p u e", u=2).unsqueeze(1).to_broadcast([P, P * n_j, 2, 2]),
+                        op=MULT,
+                    )
+
+                add(("wide", w, c), [], widen, BEHIND if w == 0 else 70 * w + 30 * c)
+                add(("turned", w, c), [("wide", w, c)], turn, BEHIND if w == 0 else 65 + 70 * w + 70 * c)
+                add(("scaled", w, c), [("turned", w, c)] + ([("scaled", w, 0)] if c > 0 else []), scale)
+
+            n_quants = n_pieces if w == 0 else 1
+            for c in range(n_quants):
+
+                def quantise(w=w, c=c, n_quants=n_quants):
+                    lo, hi = 512 // n_quants * c, 512 // n_quants * (c + 1)
+                    nc.vector.quantize_mx(out=hq[w][:, lo:hi].bitcast(FP8X4), scales=hq_scale[w][:, lo:hi], in_=scaled[w][:, 4 * lo : 4 * hi])
+
+                add(("quantised", w, c), [("scaled", w, c if w == 0 else 1)], quantise)
+
+        def quantised(w):
+            return [("quantised", w, c) for c in range(4 if w == 0 else 1)]
+
+        for w in range(CHUNKS):
             h, q = w // 4, w % 4
-            if q == 1:
-                cv[h, rt] = work.tile([128, 512], F32, name=f"cv{rt}", bufs=2)
-                o, i1 = cv[h, rt], wv[w - 1, rt]
-            else:
-                dv[h, rt] = work.tile([128, 512], F32, name=f"dv{rt % 4}", bufs=2)
-                o, i1 = dv[h, rt], cv[h, rt]
-            nc.vector.scalar_tensor_tensor(out=o[:], in0=mm[w, rt][:], scalar=bneg[:, rt:rt + 1], in1=i1[:], op0=MAX, op1=ADD)
+            for j in range(4):
 
-        def merge_g(w, rt):
-            h = w // 4
-            nc.gpsimd.tensor_tensor(out=cv[h, rt][:], in0=cv[h, rt][:], in1=wv[w, rt][:], op=ADD)
+                def add_linear(w=w, h=h, q=q, j=j):
+                    cols = slice(P * j, P * j + P)
+                    for g in range(GROUPS):
+                        nc.tensor.matmul_mx(
+                            out=bank(("linear", h, g))[:],
+                            lhsT=hq[w][:, cols].bitcast(FP8X4),
+                            lhsT_scale=hq_scale[w][:, cols],
+                            rhs=w3[:, 1024 * g : 1024 * g + 1024].bitcast(FP4X4),
+                            rhs_scale=w3_scale[:, 512 * g : 512 * g + 512],
+                            start=(q == 0 and j == 0),
+                            stop=(q == 3 and j == 3),
+                        )
 
-        def f2_tile(h, rt):
-            g = rt // 4
-            if (h, g) not in F2:
-                F2[h, g] = work.tile([128, 512], F32, name=f"F2{g}", bufs=2)
-            return F2[h, g][:, 128 * (rt % 4):128 * (rt % 4) + 128]
+                needs = [("quantised", 0, j)] if w == 0 else quantised(w)
+                if (q, j) != (0, 0):
+                    needs = needs + [("linear", w, j - 1) if j > 0 else ("linear", w - 1, 3)]
+                add(("linear", w, j), needs, add_linear, 229 + 65 * w + 17 * j + (25 if w == CHUNKS - 1 else 0))
 
-        def fold_g(h, rt):
-            d = dv[h, rt]
-            nc.gpsimd.tensor_tensor(out=d[:, 0:256], in0=d[:, 0:256], in1=d[:, 256:512], op=ADD)
-            nc.gpsimd.tensor_tensor(out=f2_tile(h, rt), in0=d[:, 0:128], in1=d[:, 128:256], op=ADD)
+        sums = {}
+        for w in range(CHUNKS):
+            h, q = w // 4, w % 4
+            for r in range(TILES):
 
-        def fold_v(h, rt):
-            nc.vector.tensor_reduce(out=f2_tile(h, rt), in_=dv[h, rt][:].rearrange("p (j b) -> p b j", j=4), axis=AXX, op=ADD)
+                def multiply(w=w, r=r):
+                    nc.tensor.matmul_mx(
+                        out=bank(("product", w, r))[:],
+                        lhsT=w3[:, 256 * r : 256 * r + 256].bitcast(FP4X4),
+                        lhsT_scale=w3_scale[:, P * r : P * r + P],
+                        rhs=hq[w][:].bitcast(FP8X4),
+                        rhs_scale=hq_scale[w][:],
+                        start=True,
+                        stop=True,
+                    )
 
-        def lin(m, rt):
-            g, t = rt // 4, rt % 4
-            if t == 0:
-                Lb[m, g] = paux.tile([128, 512], F32, name="aux")
-            lw, ls = w3_tile(rt)
-            for n in range(8):
-                w, j = 2 * m + n // 4, n % 4
-                nc.tensor.matmul_mx(out=Lb[m, g][:, 128 * t:128 * t + 128], lhsT=lw, lhsT_scale=ls,
-                                    rhs=hq[w][:, 128 * j:128 * j + 128].bitcast(FP8X4), rhs_scale=hs[w][:, 128 * j:128 * j + 128],
-                                    start=(n == 0), stop=(n == 7))
+                odd = w % 2
+                when = 185 + 74 * w + 20 * r + 21 * odd
+                if w == 0:
+                    when += 35
+                if w == CHUNKS - 1:
+                    when -= 10 * r
+                add(("product", w, r), quantised(w), multiply, when)
 
-        def lin_evac(m, g):
-            h = m // 2
-            if m % 2 == 0:
-                Lc[h, g] = work.tile([128, 512], F32, name=f"Lc{g}", bufs=2)
-                for t in range(4):
-                    nc.scalar.activation(out=Lc[h, g][:, 128 * t:128 * t + 128], in_=Lb[m, g][:, 128 * t:128 * t + 128], func=IDENT, bias=cb[:, 4 * g + t:4 * g + t + 1], scale=0.2)
-            else:
-                Lc2[h, g] = work.tile([128, 512], F32, name=f"Lcc{g}", bufs=2)
-                nc.vector.scalar_tensor_tensor(out=Lc2[h, g][:], in0=Lb[m, g][:], scalar=0.2, in1=Lc[h, g][:], op0=MULT, op1=ADD)
+                if odd:
 
-        xb, xq, xs, po = {}, {}, {}, {}
+                    def empty_onto(w=w, h=h, q=q, r=r):
+                        total = sums[h, r]
+                        nc.vector.scalar_tensor_tensor(out=total[:], in0=banks["product", w, r][:], scalar=b3_minus[:, r : r + 1], in1=total[:], op0=MAX, op1=ADD)
 
-        def make_x(h, g):
-            xb[h, g] = work.tile([128, 512], BF16, name="xb", align_bytes=64, bufs=2)
-            nc.vector.scalar_tensor_tensor(
-                out=xb[h, g][:].rearrange("p (b t) -> p b t", t=4),
-                in0=F2[h, g][:].rearrange("p (t b) -> p b t", t=4), scalar=0.8,
-                in1=Lc2[h, g][:].rearrange("p (t b) -> p b t", t=4), op0=MULT, op1=ADD)
+                    before = ("relu", w - 1, r) if q == 1 else ("merged", w - 1, r)
+                    add(("relu", w, r), [("product", w, r), before, "b3"], empty_onto)
+                else:
 
-        def quant_x(h, g):
-            xq[h, g] = work.tile([128, 128], U32, name="xq", align_bytes=64, bufs=4)
-            xs[h, g] = work.tile([128, 128], U8, name="xs", align_bytes=64, bufs=4)
-            nc.vector.quantize_mx(out=xq[h, g][:].bitcast(FP8X4), scales=xs[h, g][:], in_=xb[h, g][:])
+                    def empty(w=w, h=h, q=q, r=r):
+                        tile = sbuf.tile([P, BANK], F32, name=f"relu{w}_{r}")
+                        nc.scalar.activation(out=tile[:], in_=banks["product", w, r][:], func=RELU, bias=b3_column[:, r : r + 1])
+                        sums[(h, r) if q == 0 else (h, r, "second")] = tile
 
-        def final_pass(h, g):
-            if g == 0:
-                po[h] = paux.tile([128, 512], F32, name="aux")
-                lw, ls = xq0[:, 128 * h:128 * h + 128], xs0[:, 128 * h:128 * h + 128]
-            else:
-                lw, ls = xq[h, g - 1][:], xs[h, g - 1][:]
-            nc.tensor.matmul_mx(out=po[h][:], lhsT=lw.bitcast(FP8X4), lhsT_scale=ls, rhs=wf[:, g, :].bitcast(FP4X4), rhs_scale=wfs[:, g, :], start=(g == 0), stop=(g == 2))
+                    add(("relu", w, r), [("product", w, r), "b3"], empty)
+                    if q == 2:
 
-        def store(h):
-            o = work.tile([128, 512], F32, name="o", bufs=2)
-            nc.vector.tensor_tensor(out=o[:], in0=po[h][:], in1=bft[:], op=ADD)
-            nc.sync.dma_start(out=out[128 * h:128 * h + 128, :], in_=o[:])
+                        def merge(h=h, r=r):
+                            nc.gpsimd.tensor_tensor(out=sums[h, r][:], in0=sums[h, r][:], in1=sums[h, r, "second"][:], op=ADD)
 
-        def f_part():
-            t = ptr.tile([128, 512], F32, name="tp")
-            for h in range(2):
-                words = ft[h][:].bitcast(F32)
+                        add(("merged", w, r), [("relu", w - 1, r), ("relu", w, r)], merge)
+
+        for r in range(TILES):
+            for n in (256, 128):
+
+                def fold_on_gpsimd(r=r, n=n):
+                    total = sums[0, r]
+                    nc.gpsimd.tensor_tensor(out=total[:, 0:n], in0=total[:, 0:n], in1=total[:, n : 2 * n], op=ADD)
+
+                add(("folded", r, n), [("relu", 3, r) if n == 256 else ("folded", r, 256)], fold_on_gpsimd)
+
+        for h in range(HALVES):
+            for r in range(TILES):
+                g, t = r // 4, r % 4
+
+                def turn_sums(h=h, r=r, g=g, t=t):
+                    n = 1 if h == 0 else 4
+                    for i in range(n):
+                        nc.tensor.matmul(
+                            bank(("sum", h, g))[:, P * t : P * t + P],
+                            lhsT=sums[h, r][:, P * i : P * i + P],
+                            rhs=identity[:],
+                            is_transpose=True,
+                            start=(i == 0),
+                            stop=(i == n - 1),
+                        )
+
+                add(("sum", h, r), [("folded", r, 128) if h == 0 else ("relu", 7, r)], turn_sums, 1300 + 100 * h + 10 * r)
+
+        linear_part, msum, msum_turned, xq, xq_scale = {}, {}, {}, {}, {}
+        for h in range(HALVES):
+            for g in range(GROUPS):
+
+                def empty_linear(h=h, g=g):
+                    linear_part[h, g] = sbuf.tile([P, 512], F32, name=f"linear_part{h}{g}")
+                    nc.vector.scalar_tensor_tensor(out=linear_part[h, g][:], in0=banks["linear", h, g][:], scalar=SLOPE, in1=b3_share[:, 512 * g : 512 * g + 512], op0=MULT, op1=ADD)
+
+                def make_msum(h=h, g=g):
+                    msum[h, g] = sbuf.tile([P, 512], BF16, name=f"msum{h}{g}", align_bytes=64)
+                    nc.vector.scalar_tensor_tensor(out=msum[h, g][:], in0=banks["sum", h, g][:], scalar=RELU_SHARE, in1=linear_part[h, g][:], op0=MULT, op1=ADD)
+
+                def turn_msum(h=h, g=g):
+                    words = msum[h, g][:].bitcast(F32)
+                    for u in range(2):
+                        nc.tensor.transpose(bank(("msum", h, g))[:, P * u : P * u + P], words[:, u:256:2], identity[:])
+
+                def empty_msum(h=h, g=g):
+                    msum_turned[h, g] = sbuf.tile([P, 512], BF16, name=f"msum_turned{h}{g}", align_bytes=64)
+                    nc.scalar.copy(
+                        out=msum_turned[h, g][:].bitcast(F32).rearrange("p (n u) -> p n u", u=2),
+                        in_=banks["msum", h, g][:, 0:256].rearrange("p (u n) -> p n u", u=2),
+                    )
+
+                def quantise_msum(h=h, g=g):
+                    xq[h, g] = sbuf.tile([P, P], U32, name=f"xq{h}{g}", align_bytes=64)
+                    xq_scale[h, g] = sbuf.tile([P, P], U8, name=f"xq_scale{h}{g}", align_bytes=64)
+                    nc.vector.quantize_mx(out=xq[h, g][:].bitcast(FP8X4), scales=xq_scale[h, g][:], in_=msum_turned[h, g][:])
+
+                add(("linear_part", h, g), [("linear", 4 * h + 3, 3), "b3_share"], empty_linear)
+                add(("msum", h, g), [("linear_part", h, g)] + [("sum", h, 4 * g + t) for t in range(4)], make_msum)
+                add(("msum_bank", h, g), [("msum", h, g)], turn_msum, 1850 + 100 * h + 50 * g)
+                add(("msum_turned", h, g), [("msum_bank", h, g)], empty_msum)
+                add(("xq", h, g), [("msum_turned", h, g)], quantise_msum)
+
+        def turn_f():
+            for h in range(HALVES):
+                words = f_half[h][:].bitcast(F32)
                 for u in range(2):
-                    nc.tensor.transpose(t[:, 256 * u + 128 * h:256 * u + 128 * h + 128], words[:, u:256:2], ident[:])
-            nc.scalar.copy(out=fx[:].bitcast(F32).rearrange("p (r u) -> p r u", u=2), in_=t[:].rearrange("p (u r) -> p r u", u=2))
+                    at = P * (2 * u + h)
+                    nc.tensor.transpose(bank("f")[:, at : at + P], words[:, u:256:2], identity[:])
 
-        def permute(g, eng):
-            eng.tensor_copy(out=w3[g][:].rearrange("p (t m e) -> p t m e", t=4, e=2), in_=w3raw[:, 1024 * g:1024 * g + 1024].rearrange("p (m t e) -> p t m e", t=4, e=2))
+        def empty_f():
+            nc.scalar.copy(out=f_turned[:].bitcast(F32).rearrange("p (n u) -> p n u", u=2), in_=banks["f"][:].rearrange("p (u n) -> p n u", u=2))
 
-        def permute_s(g, eng):
-            eng.tensor_copy(out=w3s[g][:].rearrange("p (t m) -> p t m", t=4), in_=w3sraw[:, 512 * g:512 * g + 512].rearrange("p (m t) -> p t m", t=4))
+        def quantise_f():
+            nc.vector.quantize_mx(out=fq[:].bitcast(FP8X4), scales=fq_scale[:], in_=f_turned[:])
 
-        permute_s(0, nc.gpsimd)
-        permute(1, nc.gpsimd)
-        permute_s(1, nc.gpsimd)
-        cast(0, 0, "s")
-        cast(0, 1, "v")
-        tr(0, 0)
-        tr(0, 1)
-        permute(0, nc.vector)
+        add("f_bank", [], turn_f, 195)
+        add("f_turned", ["f_bank"], empty_f)
+        add("fq", ["f_turned"], quantise_f, 300)
 
-        for s in range(10):
-            sa, ha = 2 * ((s - 1) // 2), (s - 1) % 2
-            sb, hbk = 2 * ((s - 2) // 2) + 1, s % 2
-            m = (s - 2) // 2
-            has_a = 1 <= s <= 8
-            has_b = 2 <= s <= 9
-            fe = s < 8
-            nx = s + 1 if s + 1 < 8 else None
-            for i in range(4):
-                ra, rb = 4 * ha + i, 4 * hbk + i
-                if has_a:
-                    main(sa, ra)
-                if has_b:
-                    main(sb, rb)
-                    lin(m, rb)
-                if nx is not None and i < 2:
-                    cast(nx, i, "s")
-                if nx is not None and i >= 2:
-                    tr(nx, i - 2)
-                if s == 3 and i == 3:
-                    f_part()
-                if has_a:
-                    evac_s(sa, ra)
-                    if sa % 4 == 2:
-                        merge_g(sa, ra)
-                if fe and i < 2:
-                    mul(s, i)
-                if fe and i == 3:
-                    qz(s)
-                if has_b:
-                    evac_v(sb, rb)
-                    if sb % 4 == 3:
-                        if sb < 4:
-                            fold_g(0, rb)
-                        else:
-                            fold_v(1, rb)
-            if has_b:
-                lin_evac(m, hbk)
-            if s == 4:
-                nc.vector.quantize_mx(out=xq0[:].bitcast(FP8X4), scales=xs0[:], in_=fx[:])
-            if s == 6:
-                make_x(0, 0)
-            if s == 7:
-                quant_x(0, 0)
-                make_x(0, 1)
-            if s == 8:
-                quant_x(0, 1)
-                for g in range(3):
-                    final_pass(0, g)
-                store(0)
-                make_x(1, 0)
-            if s == 9:
-                quant_x(1, 0)
-                make_x(1, 1)
-                quant_x(1, 1)
-                for g in range(3):
-                    final_pass(1, g)
-                store(1)
+        for h in range(HALVES):
+            for s in range(3):
+
+                def multiply_x(h=h, s=s):
+                    if s == 0:
+                        rows, rows_scale = fq[:, P * h : P * h + P], fq_scale[:, P * h : P * h + P]
+                    else:
+                        rows, rows_scale = xq[h, s - 1][:], xq_scale[h, s - 1][:]
+                    nc.tensor.matmul_mx(
+                        out=bank(("out", h))[:],
+                        lhsT=rows.bitcast(FP8X4),
+                        lhsT_scale=rows_scale,
+                        rhs=wf[:, s, :].bitcast(FP4X4),
+                        rhs_scale=wf_scale[:, s, :],
+                        start=(s == 0),
+                        stop=(s == 2),
+                    )
+
+                needs = ["fq", ("xq", h, 0)] if s == 0 else [("xq", h, s - 1), ("out", h, s - 1)]
+                add(("out", h, s), needs, multiply_x, 2100 + 1000 * h + 300 * s)
+
+            def store(h=h):
+                result = sbuf.tile([P, 512], F32, name=f"result{h}")
+                nc.vector.tensor_tensor(out=result[:], in0=banks["out", h][:], in1=b_f_spread[:], op=ADD)
+                nc.sync.dma_start(out=out[P * h : P * h + P, :], in_=result[:])
+
+            add(("stored", h), [("out", h, 2)], store)
+
+        for piece in text_order(work):
+            piece["run"]()

from contextlib import ExitStack

import concourse.mybir as mybir
from concourse.masks import make_identity

F32 = mybir.dt.float32
BF16 = mybir.dt.bfloat16
U32 = mybir.dt.uint32
I32 = mybir.dt.int32
U8 = mybir.dt.uint8
FP8 = mybir.dt.float8_e4m3fn
FP8X4 = mybir.dt.float8_e4m3fn_x4
FP4X4 = mybir.dt.float4_e2m1fn_x4
ADD = mybir.AluOpType.add
MULT = mybir.AluOpType.mult
MAX = mybir.AluOpType.max
RELU = mybir.ActivationFunctionType.Relu

FLOPS = 2 * 4096 * 512 * 1024 + 2 * 256 * 1536 * 512

P = 128
HALVES = 2
CHUNKS = 8
TILES = 8
GROUPS = 2
BANK = 512
BANKS = 8

SLOPE = 0.2
RELU_SHARE = 1.0 - SLOPE
B3_SHARE = SLOPE * 16 + RELU_SHARE * 8

BEHIND = 0.0


def text_order(work):
    when = {}
    left = work
    while left:
        blocked = []
        for piece in left:
            if all(name in when for name in piece["needs"]):
                when[piece["name"]] = max([piece["when"]] + [when[name] + 0.001 for name in piece["needs"]])
            else:
                blocked.append(piece)
        left = blocked
    return sorted(work, key=lambda piece: when[piece["name"]])


def tile_nonlocalmp_pb_t_w4_kernel(tc, h2_bytes, h2_scale, F, W3_words, W3_scales, b3, Wf_words, Wf_scales, b_f, out):
    nc = tc.nc
    h2_rows = h2_bytes.rearrange("b i j k -> (b i) (j k)")
    f_rows = F.rearrange("b i d -> (b i) d")

    with ExitStack() as ctx:
        sbuf = ctx.enter_context(tc.tile_pool(name="sbuf", bufs=1))
        psum = ctx.enter_context(tc.psum_pool(name="psum", bufs=BANKS))
        ctx.enter_context(tc.manual_schedule())

        h2_codes = [sbuf.tile([P, 2048], U8, name=f"h2_codes{w}", align_bytes=64) for w in range(CHUNKS)]
        hq = [sbuf.tile([P, 512], U32, name=f"hq{w}", align_bytes=64) for w in range(CHUNKS)]
        hq_scale = [sbuf.tile([P, 512], U8, name=f"hq_scale{w}", align_bytes=64) for w in range(CHUNKS)]
        w3 = sbuf.tile([P, 2048], U8, name="w3", align_bytes=64)
        w3_scale = sbuf.tile([P, 1024], U8, name="w3_scale", align_bytes=64)
        wf = sbuf.tile([P, 3, 1024], U8, name="wf", align_bytes=64)
        wf_scale = sbuf.tile([P, 3, 512], U8, name="wf_scale", align_bytes=64)
        k_scale = sbuf.tile([P, 4], F32, name="k_scale")
        b3_rows = sbuf.tile([P, P], BF16, name="b3_rows")
        b3_rows_f32 = sbuf.tile([P, P], F32, name="b3_rows_f32")
        b3_column = sbuf.tile([P, TILES], F32, name="b3_column")
        b3_minus = sbuf.tile([P, TILES], F32, name="b3_minus")
        b3_spread = sbuf.tile([P, 1024], BF16, name="b3_spread")
        b3_share = sbuf.tile([P, 1024], F32, name="b3_share")
        b_f_spread = sbuf.tile([P, 512], BF16, name="b_f_spread")
        f_half = [sbuf.tile([P, 512], BF16, name=f"f_half{h}", align_bytes=64) for h in range(HALVES)]
        f_turned = sbuf.tile([P, 1024], BF16, name="f_turned", align_bytes=64)
        fq = sbuf.tile([P, 256], U32, name="fq", align_bytes=64)
        fq_scale = sbuf.tile([P, 256], U8, name="fq_scale", align_bytes=64)
        identity = sbuf.tile([P, P], F32, name="identity")
        dummy = sbuf.tile([P, 1], F32, name="dummy")

        nc.vector.memset(w3_scale[:].bitcast(I32), 0)
        make_identity(nc, identity[:])
        nc.vector.memset(dummy[:], 0.0)
        nc.gpsimd.memset(wf_scale[:].rearrange("p g n -> p (g n)").bitcast(I32), 0)
        nc.scalar.dma_start(out=k_scale[:], in_=h2_scale.rearrange("a b c (p t) -> p (a b c t)", t=4))
        nc.vector.memset(b3_rows[:], 0.0)
        nc.scalar.dma_start(out=b3_rows[0:TILES, :], in_=b3.rearrange("(r p) -> r p", p=P))
        nc.scalar.activation(out=dummy[:], in_=dummy[:], func=RELU)

        def load_h2(w, lo, hi):
            h, q = w // 4, w % 4
            nc.sync.dma_start(out=h2_codes[w][:, lo:hi], in_=h2_rows[P * h : P * h + P, 2048 * q + lo : 2048 * q + hi])

        load_h2(0, 0, 1024)
        load_h2(0, 1024, 2048)
        for Q in range(4):
            nc.sync.dma_start(out=w3_scale[32 * Q : 32 * Q + 4, :].bitcast(I32), in_=W3_scales[0, 4 * Q : 4 * Q + 4, :].bitcast(I32))
        nc.sync.dma_start(out=w3[:], in_=W3_words[0])
        for h in range(HALVES):
            nc.sync.dma_start(out=f_half[h][:], in_=f_rows[P * h : P * h + P, :])
        for w in range(1, CHUNKS):
            load_h2(w, 0, 2048)
        nc.sync.dma_start(out=wf[:], in_=Wf_words.rearrange("g p n -> p g n"))
        for Q in range(4):
            nc.sync.dma_start(
                out=wf_scale[32 * Q : 32 * Q + 4, :, :].bitcast(I32),
                in_=Wf_scales[:, 4 * Q : 4 * Q + 4, :].rearrange("g q n -> q g n").bitcast(I32),
            )
        nc.sync.dma_start(out=b3_spread[:], in_=b3.partition_broadcast(P))
        nc.sync.dma_start(out=b_f_spread[:], in_=b_f.partition_broadcast(P))

        work = []

        def add(name, needs, run, when=BEHIND):
            work.append({"name": name, "needs": needs, "when": when, "run": run})

        banks = {}

        def bank(name):
            if name not in banks:
                banks[name] = psum.tile([P, BANK], F32, name="bank")
            return banks[name]

        def spread_b3_share():
            nc.gpsimd.tensor_scalar(out=b3_share[:], in0=b3_spread[:], scalar1=B3_SHARE, scalar2=0.0, op0=MULT, op1=ADD)

        def widen_b3_rows():
            nc.vector.tensor_copy(out=b3_rows_f32[:], in_=b3_rows[:])

        def turn_b3_rows():
            nc.tensor.transpose(bank("b3")[:, 0:P], b3_rows_f32[:], identity[:])

        def empty_b3_bank():
            nc.vector.tensor_copy(out=b3_column[:], in_=banks["b3"][:, 0:TILES])
            nc.vector.tensor_scalar(out=b3_minus[:], in0=banks["b3"][:, 0:TILES], scalar1=-1.0, scalar2=None, op0=MULT)

        add("b3_share", [], spread_b3_share)
        add("b3_widened", [("quantised", 0, 0)], widen_b3_rows)
        add("b3_turned", ["b3_widened"], turn_b3_rows)
        add("b3", ["b3_turned"], empty_b3_bank)

        wide, scaled = {}, {}
        for w in range(CHUNKS):
            n_pieces = 4 if w == 0 else 2
            n_j = 4 // n_pieces
            for c in range(n_pieces):
                lo, hi = 512 * n_j * c, 512 * n_j * (c + 1)

                def widen(w=w, c=c, lo=lo, hi=hi):
                    wide[w, c] = sbuf.tile([P, hi - lo], BF16, name=f"wide{w}_{c}", align_bytes=64)
                    codes = h2_codes[w][:, lo:hi].bitcast(FP8)
                    if w == 0 and c % 2 == 0:
                        nc.vector.tensor_copy(out=wide[w, c][:], in_=codes)
                    else:
                        nc.scalar.copy(out=wide[w, c][:], in_=codes)

                def turn(w=w, c=c, n_j=n_j):
                    words = wide[w, c][:].bitcast(F32)
                    for j in range(n_j):
                        for u in range(2):
                            at = P * (n_j * u + j)
                            nc.tensor.transpose(bank(("turned", w, c))[:, at : at + P], words[:, 256 * j + u : 256 * j + 256 : 2], identity[:])

                def scale(w=w, c=c, lo=lo, hi=hi, n_j=n_j):
                    if c == 0:
                        scaled[w] = sbuf.tile([P, 2048], BF16, name=f"scaled{w}", align_bytes=64)
                    nc.vector.tensor_tensor(
                        out=scaled[w][:, lo:hi].rearrange("p (n u e) -> p n u e", u=2, e=2),
                        in0=banks["turned", w, c][:, 0 : 256 * n_j].bitcast(BF16).rearrange("p (u n e) -> p n u e", u=2, e=2),
                        in1=k_scale[:].rearrange("p (u e) -> p u e", u=2).unsqueeze(1).to_broadcast([P, P * n_j, 2, 2]),
                        op=MULT,
                    )

                add(("wide", w, c), [], widen, BEHIND if w == 0 else 70 * w + 30 * c)
                add(("turned", w, c), [("wide", w, c)], turn, BEHIND if w == 0 else 65 + 70 * w + 70 * c)
                add(("scaled", w, c), [("turned", w, c)] + ([("scaled", w, 0)] if c > 0 else []), scale)

            n_quants = n_pieces if w == 0 else 1
            for c in range(n_quants):

                def quantise(w=w, c=c, n_quants=n_quants):
                    lo, hi = 512 // n_quants * c, 512 // n_quants * (c + 1)
                    nc.vector.quantize_mx(out=hq[w][:, lo:hi].bitcast(FP8X4), scales=hq_scale[w][:, lo:hi], in_=scaled[w][:, 4 * lo : 4 * hi])

                add(("quantised", w, c), [("scaled", w, c if w == 0 else 1)], quantise)

        def quantised(w):
            return [("quantised", w, c) for c in range(4 if w == 0 else 1)]

        for w in range(CHUNKS):
            h, q = w // 4, w % 4
            for j in range(4):

                def add_linear(w=w, h=h, q=q, j=j):
                    cols = slice(P * j, P * j + P)
                    for g in range(GROUPS):
                        nc.tensor.matmul_mx(
                            out=bank(("linear", h, g))[:],
                            lhsT=hq[w][:, cols].bitcast(FP8X4),
                            lhsT_scale=hq_scale[w][:, cols],
                            rhs=w3[:, 1024 * g : 1024 * g + 1024].bitcast(FP4X4),
                            rhs_scale=w3_scale[:, 512 * g : 512 * g + 512],
                            start=(q == 0 and j == 0),
                            stop=(q == 3 and j == 3),
                        )

                needs = [("quantised", 0, j)] if w == 0 else quantised(w)
                if (q, j) != (0, 0):
                    needs = needs + [("linear", w, j - 1) if j > 0 else ("linear", w - 1, 3)]
                add(("linear", w, j), needs, add_linear, 229 + 65 * w + 17 * j + (25 if w == CHUNKS - 1 else 0))

        sums = {}
        for w in range(CHUNKS):
            h, q = w // 4, w % 4
            for r in range(TILES):

                def multiply(w=w, r=r):
                    nc.tensor.matmul_mx(
                        out=bank(("product", w, r))[:],
                        lhsT=w3[:, 256 * r : 256 * r + 256].bitcast(FP4X4),
                        lhsT_scale=w3_scale[:, P * r : P * r + P],
                        rhs=hq[w][:].bitcast(FP8X4),
                        rhs_scale=hq_scale[w][:],
                        start=True,
                        stop=True,
                    )

                odd = w % 2
                when = 185 + 74 * w + 20 * r + 21 * odd
                if w == 0:
                    when += 35
                if w == CHUNKS - 1:
                    when -= 10 * r
                add(("product", w, r), quantised(w), multiply, when)

                if odd:

                    def empty_onto(w=w, h=h, q=q, r=r):
                        total = sums[h, r]
                        nc.vector.scalar_tensor_tensor(out=total[:], in0=banks["product", w, r][:], scalar=b3_minus[:, r : r + 1], in1=total[:], op0=MAX, op1=ADD)

                    before = ("relu", w - 1, r) if q == 1 else ("merged", w - 1, r)
                    add(("relu", w, r), [("product", w, r), before, "b3"], empty_onto)
                else:

                    def empty(w=w, h=h, q=q, r=r):
                        tile = sbuf.tile([P, BANK], F32, name=f"relu{w}_{r}")
                        nc.scalar.activation(out=tile[:], in_=banks["product", w, r][:], func=RELU, bias=b3_column[:, r : r + 1])
                        sums[(h, r) if q == 0 else (h, r, "second")] = tile

                    add(("relu", w, r), [("product", w, r), "b3"], empty)
                    if q == 2:

                        def merge(h=h, r=r):
                            nc.gpsimd.tensor_tensor(out=sums[h, r][:], in0=sums[h, r][:], in1=sums[h, r, "second"][:], op=ADD)

                        add(("merged", w, r), [("relu", w - 1, r), ("relu", w, r)], merge)

        for r in range(TILES):
            for n in (256, 128):

                def fold_on_gpsimd(r=r, n=n):
                    total = sums[0, r]
                    nc.gpsimd.tensor_tensor(out=total[:, 0:n], in0=total[:, 0:n], in1=total[:, n : 2 * n], op=ADD)

                add(("folded", r, n), [("relu", 3, r) if n == 256 else ("folded", r, 256)], fold_on_gpsimd)

        for h in range(HALVES):
            for r in range(TILES):
                g, t = r // 4, r % 4

                def turn_sums(h=h, r=r, g=g, t=t):
                    n = 1 if h == 0 else 4
                    for i in range(n):
                        nc.tensor.matmul(
                            bank(("sum", h, g))[:, P * t : P * t + P],
                            lhsT=sums[h, r][:, P * i : P * i + P],
                            rhs=identity[:],
                            is_transpose=True,
                            start=(i == 0),
                            stop=(i == n - 1),
                        )

                add(("sum", h, r), [("folded", r, 128) if h == 0 else ("relu", 7, r)], turn_sums, 1300 + 100 * h + 10 * r)

        linear_part, msum, msum_turned, xq, xq_scale = {}, {}, {}, {}, {}
        for h in range(HALVES):
            for g in range(GROUPS):

                def empty_linear(h=h, g=g):
                    linear_part[h, g] = sbuf.tile([P, 512], F32, name=f"linear_part{h}{g}")
                    nc.vector.scalar_tensor_tensor(out=linear_part[h, g][:], in0=banks["linear", h, g][:], scalar=SLOPE, in1=b3_share[:, 512 * g : 512 * g + 512], op0=MULT, op1=ADD)

                def make_msum(h=h, g=g):
                    msum[h, g] = sbuf.tile([P, 512], BF16, name=f"msum{h}{g}", align_bytes=64)
                    nc.vector.scalar_tensor_tensor(out=msum[h, g][:], in0=banks["sum", h, g][:], scalar=RELU_SHARE, in1=linear_part[h, g][:], op0=MULT, op1=ADD)

                def turn_msum(h=h, g=g):
                    words = msum[h, g][:].bitcast(F32)
                    for u in range(2):
                        nc.tensor.transpose(bank(("msum", h, g))[:, P * u : P * u + P], words[:, u:256:2], identity[:])

                def empty_msum(h=h, g=g):
                    msum_turned[h, g] = sbuf.tile([P, 512], BF16, name=f"msum_turned{h}{g}", align_bytes=64)
                    nc.scalar.copy(
                        out=msum_turned[h, g][:].bitcast(F32).rearrange("p (n u) -> p n u", u=2),
                        in_=banks["msum", h, g][:, 0:256].rearrange("p (u n) -> p n u", u=2),
                    )

                def quantise_msum(h=h, g=g):
                    xq[h, g] = sbuf.tile([P, P], U32, name=f"xq{h}{g}", align_bytes=64)
                    xq_scale[h, g] = sbuf.tile([P, P], U8, name=f"xq_scale{h}{g}", align_bytes=64)
                    nc.vector.quantize_mx(out=xq[h, g][:].bitcast(FP8X4), scales=xq_scale[h, g][:], in_=msum_turned[h, g][:])

                add(("linear_part", h, g), [("linear", 4 * h + 3, 3), "b3_share"], empty_linear)
                add(("msum", h, g), [("linear_part", h, g)] + [("sum", h, 4 * g + t) for t in range(4)], make_msum)
                add(("msum_bank", h, g), [("msum", h, g)], turn_msum, 1850 + 100 * h + 50 * g)
                add(("msum_turned", h, g), [("msum_bank", h, g)], empty_msum)
                add(("xq", h, g), [("msum_turned", h, g)], quantise_msum)

        def turn_f():
            for h in range(HALVES):
                words = f_half[h][:].bitcast(F32)
                for u in range(2):
                    at = P * (2 * u + h)
                    nc.tensor.transpose(bank("f")[:, at : at + P], words[:, u:256:2], identity[:])

        def empty_f():
            nc.scalar.copy(out=f_turned[:].bitcast(F32).rearrange("p (n u) -> p n u", u=2), in_=banks["f"][:].rearrange("p (u n) -> p n u", u=2))

        def quantise_f():
            nc.vector.quantize_mx(out=fq[:].bitcast(FP8X4), scales=fq_scale[:], in_=f_turned[:])

        add("f_bank", [], turn_f, 195)
        add("f_turned", ["f_bank"], empty_f)
        add("fq", ["f_turned"], quantise_f, 300)

        for h in range(HALVES):
            for s in range(3):

                def multiply_x(h=h, s=s):
                    if s == 0:
                        rows, rows_scale = fq[:, P * h : P * h + P], fq_scale[:, P * h : P * h + P]
                    else:
                        rows, rows_scale = xq[h, s - 1][:], xq_scale[h, s - 1][:]
                    nc.tensor.matmul_mx(
                        out=bank(("out", h))[:],
                        lhsT=rows.bitcast(FP8X4),
                        lhsT_scale=rows_scale,
                        rhs=wf[:, s, :].bitcast(FP4X4),
                        rhs_scale=wf_scale[:, s, :],
                        start=(s == 0),
                        stop=(s == 2),
                    )

                needs = ["fq", ("xq", h, 0)] if s == 0 else [("xq", h, s - 1), ("out", h, s - 1)]
                add(("out", h, s), needs, multiply_x, 2100 + 1000 * h + 300 * s)

            def store(h=h):
                result = sbuf.tile([P, 512], F32, name=f"result{h}")
                nc.vector.tensor_tensor(out=result[:], in0=banks["out", h][:], in1=b_f_spread[:], op=ADD)
                nc.sync.dma_start(out=out[P * h : P * h + P, :], in_=result[:])

            add(("stored", h), [("out", h, 2)], store)

        for piece in text_order(work):
            piece["run"]()
